import numpy as np
import ml_dtypes


def mxq(x, axis, fmt="e4m3"):
    dtype, down = {"e4m3": (ml_dtypes.float8_e4m3fn, 7), "e5m2": (ml_dtypes.float8_e5m2, 14)}[fmt]
    v = np.moveaxis(np.asarray(x, np.float32).astype(ml_dtypes.bfloat16).astype(np.float64), axis, -1)
    blocks = v.reshape(v.shape[:-1] + (-1, 32))
    amax = np.abs(blocks).max(-1, keepdims=True)
    byte = np.maximum(np.where(amax > 0, np.frexp(amax)[1] - 1 + 127, 0) - down, 1)
    scale = np.exp2(byte - 127.0)
    codes = (blocks / scale).astype(np.float32).astype(dtype).astype(np.float64)
    return np.moveaxis((codes * scale).reshape(v.shape), -1, axis)


WIDE = False


def mx_kscale(k):
    if not WIDE:
        return np.ones(k)
    levels = np.array([10, -10, 5, -5, 0])
    a = np.random.permutation(np.resize(levels, k // 512 * 4)).reshape(k // 512, 4)
    idx = np.arange(k)
    return np.exp2(a[idx // 512, idx % 128 // 32])


BF16 = ml_dtypes.bfloat16


def bf(x):
    return np.asarray(x, np.float32).astype(BF16)


def f64(x):
    return np.asarray(x).astype(np.float64)


B, S, DV, DL, D = 8, 512, 1024, 1024, 512
EPS = 1e-5
TEMPERATURE = 0.07


def layernorm(x, g, b):
    m = x.mean(-1, keepdims=True)
    v = np.square(x - m).mean(-1, keepdims=True)
    return (x - m) / np.sqrt(v + EPS) * g + b


def setup_inputs():
    s, u = mx_kscale(DV), mx_kscale(DL)
    return {
        'vision_features': bf(np.random.standard_normal((B, S, DV)) * s),
        'language_features': bf(np.random.standard_normal((B, S, DL)) * u),
        'vW': bf(np.random.standard_normal((DV, D)) / np.sqrt(DV) / s[:, None]),
        'vb': bf(0.1 * np.random.standard_normal(D)),
        'vg': bf(1.0 + 0.1 * np.random.standard_normal(D)),
        'vbeta': bf(0.1 * np.random.standard_normal(D)),
        'lW': bf(np.random.standard_normal((DL, D)) / np.sqrt(DL) / u[:, None]),
        'lb': bf(0.1 * np.random.standard_normal(D)),
        'lg': bf(1.0 + 0.1 * np.random.standard_normal(D)),
        'lbeta': bf(0.1 * np.random.standard_normal(D)),
        'claw': bf((np.random.standard_normal((D, D)) + 0.15) / np.sqrt(D)),
    }


def reference(vision_features, language_features, vW, vb, vg, vbeta, lW, lb, lg, lbeta, claw):
    hv = (mxq(f64(vision_features), 2, 'e4m3') @ mxq(f64(vW), 0, 'e4m3')) + f64(vb)
    vp = np.maximum(layernorm(hv, f64(vg), f64(vbeta)), 0.0)
    hl = (mxq(f64(language_features), 2, 'e4m3') @ mxq(f64(lW), 0, 'e4m3')) + f64(lb)
    lp = np.maximum(layernorm(hl, f64(lg), f64(lbeta)), 0.0)
    sim = (mxq(vp, 2, 'e4m3') @ mxq(lp, 2, 'e4m3').transpose(0, 2, 1)) * (f64(claw).mean() / TEMPERATURE)
    e = np.exp(sim - sim.max(-1, keepdims=True))
    return e / e.sum(-1, keepdims=True)

@@ -1,0 +1,365 @@
+from contextlib import ExitStack
+
+import concourse.mybir as mybir
+from concourse.masks import make_identity
+
+F32 = mybir.dt.float32
+BF16 = mybir.dt.bfloat16
+U32 = mybir.dt.uint32
+U8 = mybir.dt.uint8
+FP8X4 = mybir.dt.float8_e4m3fn_x4
+ALU = mybir.AluOpType
+ACT = mybir.ActivationFunctionType
+AXIS_X = mybir.AxisListType.X
+
+B, S, K, D = 8, 512, 1024, 512
+EPS = 1e-5
+TEMPERATURE = 0.07
+
+P = 128
+PACK = 4
+K_PASS = P * PACK
+PASSES = K // K_PASS
+TILES = S // P
+STREAMS = 2
+GROUPS = B * STREAMS
+WORDS = K // 2
+
+FLOPS = 2 * STREAMS * B * S * K * D + 2 * B * S * S * D
+
+
+def tile_clawmatrix_pa_t_kernel(
+    tc, vision_features, language_features, vW, vb, vg, vbeta, lW, lb, lg, lbeta, claw, out
+):
+    nc = tc.nc
+    features = [vision_features, language_features]
+    weights = [vW, lW]
+    biases = [vb, lb]
+
+    with ExitStack() as ctx:
+        const = ctx.enter_context(tc.tile_pool(name="const", bufs=1))
+        setup = ctx.enter_context(tc.tile_pool(name="setup", bufs=2))
+        x_pool = ctx.enter_context(tc.tile_pool(name="x", bufs=3))
+        xq_pool = ctx.enter_context(tc.tile_pool(name="xq", bufs=4))
+        z_pool = ctx.enter_context(tc.tile_pool(name="z", bufs=3))
+        stat_pool = ctx.enter_context(tc.tile_pool(name="stat", bufs=4))
+        scrap_pool = ctx.enter_context(tc.tile_pool(name="scrap", bufs=4))
+        y_pool = ctx.enter_context(tc.tile_pool(name="y", bufs=2))
+        soft_pool = ctx.enter_context(tc.tile_pool(name="soft", bufs=6))
+        psum = ctx.enter_context(tc.psum_pool(name="psum", bufs=2))
+
+        x_loaded, x_quantised, w_loaded, w_quantised = {}, {}, {}, {}
+        summed, rstds, normeds, rectified, y_quantised = {}, {}, {}, {}, {}
+        sims, logits, exponentials = {}, {}, {}
+
+        def load_features(group):
+            batch, stream = divmod(group, STREAMS)
+            x_in = x_pool.tile([P, TILES * K], BF16, tag="x_in")
+            nc.sync.dma_start(
+                out=x_in[:].rearrange("p (r k) -> p r k", r=TILES),
+                in_=features[stream][batch].rearrange("(r p) k -> p r k", p=P),
+            )
+            x_loaded[group] = x_in
+
+        def load_weight(stream):
+            w_raw = setup.tile([P, PASSES * PACK * D], BF16, tag="w_raw")
+            nc.sync.dma_start(
+                out=w_raw[:].rearrange("q (a c) -> q a c", c=2 * D),
+                in_=weights[stream].rearrange("(a q e) c -> q a (e c)", q=P, e=2),
+            )
+            w_loaded[stream] = w_raw
+
+        bias_rows = []
+        for stream in range(STREAMS):
+            load_features(stream)
+            load_weight(stream)
+            bias_row = const.tile([P, D], BF16, name="bias_row%d" % stream)
+            nc.sync.dma_start(out=bias_row[:], in_=biases[stream].partition_broadcast(P))
+            bias_rows.append(bias_row)
+        gain_rows = const.tile([P, P], BF16)
+        nc.vector.memset(gain_rows[:], 0.0)
+        for j, vector in enumerate([vg, vbeta, lg, lbeta]):
+            nc.sync.dma_start(
+                out=gain_rows[PACK * j : PACK * (j + 1), :],
+                in_=vector.rearrange("(t c) -> t c", t=PACK),
+            )
+        claw_sb = const.tile([P, D * D // P], BF16)
+        nc.sync.dma_start(out=claw_sb[:], in_=claw.rearrange("(p a) c -> p (a c)", p=P))
+
+        ident = const.tile([P, P], F32)
+        make_identity(nc, ident[:])
+        neg_half = const.tile([P, TILES], F32)
+        nc.vector.memset(neg_half[:], -0.5)
+        gains = const.tile([P, 4 * PACK], F32)
+        neg_scale = const.tile([P, 1], F32)
+
+        def prepare_gains():
+            gain_rows_f32 = const.tile([P, P], F32)
+            nc.vector.tensor_copy(out=gain_rows_f32[:], in_=gain_rows[:])
+            gains_ps = psum.tile([P, P], F32, tag="yt")
+            nc.tensor.transpose(out=gains_ps[:], in_=gain_rows_f32[:], identity=ident[:])
+            nc.vector.tensor_copy(out=gains[:], in_=gains_ps[:, 0 : 4 * PACK])
+
+        def prepare_scale():
+            partial = const.tile([P, 1], F32)
+            nc.vector.tensor_reduce(out=partial[:], in_=claw_sb[:], axis=AXIS_X, op=ALU.add)
+            repeated = const.tile([P, P], F32)
+            nc.vector.tensor_copy(out=repeated[:], in_=partial[:].to_broadcast([P, P]))
+            partials_ps = psum.tile([P, P], F32, tag="yt")
+            nc.tensor.transpose(out=partials_ps[:], in_=repeated[:], identity=ident[:])
+            claw_sum = const.tile([P, 1], F32)
+            nc.vector.tensor_reduce(out=claw_sum[:], in_=partials_ps[:], axis=AXIS_X, op=ALU.add)
+            nc.vector.tensor_scalar(
+                out=neg_scale[:],
+                in0=claw_sum[:],
+                scalar1=-1.0 / (D * D * TEMPERATURE),
+                scalar2=None,
+                op0=ALU.mult,
+            )
+
+        def quantise_weight(stream):
+            codes = const.tile([P, PASSES * D], U32, name="w_codes%d" % stream, align_bytes=64)
+            scales = const.tile([P, PASSES * D], U8, name="w_scales%d" % stream, align_bytes=64)
+            for g in range(PASSES):
+                w_grouped = setup.tile([P, D * PACK], BF16, tag="w_grouped", align_bytes=64)
+                nc.vector.tensor_copy(
+                    out=w_grouped[:].rearrange("p (c i t) -> p c t i", i=4, t=PACK),
+                    in_=w_loaded[stream][:, g * PACK * D : (g + 1) * PACK * D].rearrange(
+                        "p (t c i) -> p c t i", t=PACK, i=4
+                    ),
+                )
+                nc.vector.quantize_mx(
+                    out=codes[:, g * D : (g + 1) * D].bitcast(FP8X4),
+                    scales=scales[:, g * D : (g + 1) * D],
+                    in_=w_grouped[:],
+                )
+            w_quantised[stream] = (codes, scales)
+
+        def transpose_features(group):
+            x_words = x_loaded[group][:].bitcast(F32)
+            halves = []
+            for half in range(2):
+                x_grouped = xq_pool.tile(
+                    [P, 2 * PASSES * P * PACK], BF16, tag="x_grouped", align_bytes=64
+                )
+                x_grouped_words = x_grouped[:].bitcast(F32)
+                for i in range(2):
+                    r = 2 * half + i
+                    xt = psum.tile([P, WORDS], F32, tag="xt")
+                    for j in range(WORDS // P):
+                        nc.tensor.transpose(
+                            out=xt[:, j * P : (j + 1) * P],
+                            in_=x_words[:, r * WORDS + j * P : r * WORDS + (j + 1) * P],
+                            identity=ident[:],
+                        )
+                    nc.scalar.copy(
+                        out=x_grouped_words[:, i * WORDS : (i + 1) * WORDS].rearrange(
+                            "p (g c u) -> p g c u", g=PASSES, u=2
+                        ),
+                        in_=xt[:].rearrange("p (g u c) -> p g c u", g=PASSES, u=2),
+                    )
+                codes = xq_pool.tile([P, 2 * PASSES * P], U32, tag="x_codes", align_bytes=64)
+                scales = xq_pool.tile([P, 2 * PASSES * P], U8, tag="x_scales", align_bytes=64)
+                nc.vector.quantize_mx(
+                    out=codes[:].bitcast(FP8X4), scales=scales[:], in_=x_grouped[:]
+                )
+                halves.append((codes, scales))
+            x_quantised[group] = halves
+
+        def project(group):
+            stream = group % STREAMS
+            w_codes, w_scales = w_quantised[stream]
+            z = z_pool.tile([P, TILES, D], F32, tag="z")
+            sums = stat_pool.tile([P, TILES], F32, tag="sums")
+            for r in range(TILES):
+                codes, scales = x_quantised[group][r // 2]
+                h = psum.tile([P, D], F32, tag="h")
+                for g in range(PASSES):
+                    cols = slice(((r % 2) * PASSES + g) * P, ((r % 2) * PASSES + g + 1) * P)
+                    nc.tensor.matmul_mx(
+                        out=h[:],
+                        lhsT=codes[:, cols].bitcast(FP8X4),
+                        lhsT_scale=scales[:, cols],
+                        rhs=w_codes[:, g * D : (g + 1) * D].bitcast(FP8X4),
+                        rhs_scale=w_scales[:, g * D : (g + 1) * D],
+                        start=(g == 0),
+                        stop=(g == PASSES - 1),
+                    )
+                nc.vector.scalar_tensor_tensor(
+                    out=z[:, r, :],
+                    in0=h[:],
+                    scalar=1.0,
+                    in1=bias_rows[stream][:],
+                    op0=ALU.mult,
+                    op1=ALU.add,
+                    accum_out=sums[:, r : r + 1],
+                )
+            neg_mean = stat_pool.tile([P, TILES], F32, tag="neg_mean")
+            nc.vector.tensor_scalar(
+                out=neg_mean[:], in0=sums[:], scalar1=-1.0 / D, scalar2=None, op0=ALU.mult
+            )
+            summed[group] = (z, neg_mean)
+
+        def variance(group):
+            z, neg_mean = summed[group]
+            square_sums = stat_pool.tile([P, TILES], F32, tag="square_sums")
+            for r in range(TILES):
+                squares = scrap_pool.tile([P, D], BF16, tag="squares")
+                nc.scalar.activation(
+                    out=squares[:],
+                    in_=z[:, r, :],
+                    func=ACT.Square,
+                    bias=neg_mean[:, r : r + 1],
+                    scale=1.0,
+                    accum_out=square_sums[:, r : r + 1],
+                )
+            var_eps = stat_pool.tile([P, TILES], F32, tag="var_eps")
+            nc.gpsimd.tensor_scalar(
+                out=var_eps[:],
+                in0=square_sums[:],
+                scalar1=1.0 / D,
+                scalar2=EPS,
+                op0=ALU.mult,
+                op1=ALU.add,
+            )
+            rstd = stat_pool.tile([P, TILES], F32, tag="rstd")
+            nc.gpsimd.tensor_tensor(out=rstd[:], in0=var_eps[:], in1=neg_half[:], op=ALU.pow)
+            rstds[group] = rstd
+
+        def normalise(group):
+            z, neg_mean = summed[group]
+            normed = y_pool.tile([P, TILES, D], F32, tag="normed")
+            for r in range(TILES):
+                nc.vector.tensor_scalar(
+                    out=normed[:, r, :],
+                    in0=z[:, r, :],
+                    scalar1=neg_mean[:, r : r + 1],
+                    scalar2=rstds[group][:, r : r + 1],
+                    op0=ALU.add,
+                    op1=ALU.mult,
+                )
+            normeds[group] = normed
+
+        def rectify(group):
+            first = 2 * PACK * (group % STREAMS)
+            planes = y_pool.tile([P, PACK, S], BF16, tag="planes")
+            for t in range(PACK):
+                yt = psum.tile([P, S], F32, tag="yt")
+                for r in range(TILES):
+                    nc.tensor.transpose(
+                        out=yt[:, r * P : (r + 1) * P],
+                        in_=normeds[group][:, r, t * P : (t + 1) * P],
+                        identity=ident[:],
+                    )
+                nc.scalar.activation(
+                    out=planes[:, t, :],
+                    in_=yt[:],
+                    func=ACT.Relu,
+                    bias=gains[:, first + PACK + t : first + PACK + t + 1],
+                    scale=gains[:, first + t : first + t + 1],
+                )
+            rectified[group] = planes
+
+        def quantise_rectified(group):
+            y_grouped = y_pool.tile([P, S * PACK], BF16, tag="y_grouped", align_bytes=64)
+            nc.vector.tensor_copy(
+                out=y_grouped[:].rearrange("p (c i t) -> p c t i", i=4, t=PACK),
+                in_=rectified[group][:].rearrange("p t (c i) -> p c t i", i=4),
+            )
+            stream = group % STREAMS
+            codes = y_pool.tile([P, S], U32, tag="y_codes%d" % stream, align_bytes=64)
+            scales = y_pool.tile([P, S], U8, tag="y_scales%d" % stream, align_bytes=64)
+            nc.vector.quantize_mx(out=codes[:].bitcast(FP8X4), scales=scales[:], in_=y_grouped[:])
+            y_quantised[group] = (codes, scales)
+
+        def similarity(batch, r):
+            v_codes, v_scales = y_quantised[STREAMS * batch]
+            l_codes, l_scales = y_quantised[STREAMS * batch + 1]
+            sim = psum.tile([P, S], F32, tag="sim")
+            nc.tensor.matmul_mx(
+                out=sim[:],
+                lhsT=v_codes[:, r * P : (r + 1) * P].bitcast(FP8X4),
+                lhsT_scale=v_scales[:, r * P : (r + 1) * P],
+                rhs=l_codes[:].bitcast(FP8X4),
+                rhs_scale=l_scales[:],
+                start=True,
+                stop=True,
+            )
+            sims[(batch, r)] = sim
+
+        def scale_logits(batch, r):
+            neg_logits = soft_pool.tile([P, S], F32, tag="neg_logits")
+            neg_max = soft_pool.tile([P, 1], F32, tag="neg_max")
+            nc.vector.tensor_scalar(
+                out=neg_logits[:],
+                in0=sims[(batch, r)][:],
+                scalar1=neg_scale[:],
+                scalar2=None,
+                op0=ALU.mult,
+                op1=ALU.min,
+                accum_out=neg_max[:],
+            )
+            logits[(batch, r)] = (neg_logits, neg_max)
+
+        def exponentiate(batch, r):
+            neg_logits, neg_max = logits[(batch, r)]
+            probs = soft_pool.tile([P, S], F32, tag="probs")
+            row_sum = soft_pool.tile([P, 1], F32, tag="row_sum")
+            nc.scalar.activation(
+                out=probs[:],
+                in_=neg_logits[:],
+                func=ACT.Exp,
+                bias=neg_max[:],
+                scale=-1.0,
+                accum_out=row_sum[:],
+            )
+            exponentials[(batch, r)] = (probs, row_sum)
+
+        def store_probabilities(batch, r):
+            probs, row_sum = exponentials[(batch, r)]
+            inverse = soft_pool.tile([P, 1], F32, tag="inverse")
+            nc.vector.reciprocal(out=inverse[:], in_=row_sum[:])
+            nc.vector.tensor_scalar(
+                out=probs[:], in0=probs[:], scalar1=inverse[:], scalar2=None, op0=ALU.mult
+            )
+            nc.sync.dma_start(out=out[batch, r * P : (r + 1) * P, :], in_=probs[:])
+
+        def tile_pair(n):
+            if not 0 <= n < GROUPS:
+                return []
+            return [(n // 2, 2 * (n % 2)), (n // 2, 2 * (n % 2) + 1)]
+
+        def in_range(group):
+            return 0 <= group < GROUPS
+
+        for step in range(GROUPS + 5):
+            if in_range(step + 2):
+                load_features(step + 2)
+            if in_range(step - 3):
+                quantise_rectified(step - 3)
+            if in_range(step - 2):
+                normalise(step - 2)
+            if step == 0:
+                quantise_weight(0)
+            if in_range(step):
+                transpose_features(step)
+            for batch, r in tile_pair(step - 5):
+                exponentiate(batch, r)
+            for batch, r in tile_pair(step - 4):
+                similarity(batch, r)
+            if in_range(step):
+                project(step)
+            for batch, r in tile_pair(step - 4):
+                scale_logits(batch, r)
+            for batch, r in tile_pair(step - 5):
+                store_probabilities(batch, r)
+            if step == 0:
+                quantise_weight(1)
+            if in_range(step - 1):
+                variance(step - 1)
+            if in_range(step - 2):
+                rectify(step - 2)
+            if step == 0:
+                prepare_gains()
+            if step == 1:
+                prepare_scale()

@@ -22,76 +22,114 @@ K_PASS = P * PACK
 PASSES = K // K_PASS
 TILES = S // P
 STREAMS = 2
+LANGUAGE, VISION = 0, 1
 GROUPS = B * STREAMS
+ALL_TILES = GROUPS * TILES
 WORDS = K // 2
 
 FLOPS = 2 * STREAMS * B * S * K * D + 2 * B * S * S * D
+
+LAG_QUANT = 2
+LAG_PROJECT = 2
+LAG_SUM = 3
+LAG_SQUARE = 5
+LAG_NORM = 10
+LAG_TURN = 14
+LAG_RELU = 14
+LAG_REGROUP = 19
+LAG_YQUANT = 20
+LAG_SIM = 21
+LAG_LOGITS = 22
+LAG_EXP = 23
+LAG_STORE = 25
+LOAD_AHEAD = 8
+W_PARTS = 4
 
 
 def tile_clawmatrix_pa_t_kernel(
     tc, vision_features, language_features, vW, vb, vg, vbeta, lW, lb, lg, lbeta, claw, out
 ):
     nc = tc.nc
-    features = [vision_features, language_features]
-    weights = [vW, lW]
-    biases = [vb, lb]
+    features = [language_features, vision_features]
+    weights = [lW, vW]
+    biases = [lb, vb]
 
     with ExitStack() as ctx:
         const = ctx.enter_context(tc.tile_pool(name="const", bufs=1))
-        setup = ctx.enter_context(tc.tile_pool(name="setup", bufs=2))
-        x_pool = ctx.enter_context(tc.tile_pool(name="x", bufs=3))
-        xq_pool = ctx.enter_context(tc.tile_pool(name="xq", bufs=4))
-        z_pool = ctx.enter_context(tc.tile_pool(name="z", bufs=3))
+        setup = ctx.enter_context(tc.tile_pool(name="setup", bufs=STREAMS * PASSES))
+        x_pool = ctx.enter_context(tc.tile_pool(name="x", bufs=16))
+        xq_pool = ctx.enter_context(tc.tile_pool(name="xq", bufs=6))
+        z_pool = ctx.enter_context(tc.tile_pool(name="z", bufs=10))
+        n_pool = ctx.enter_context(tc.tile_pool(name="n", bufs=14))
         stat_pool = ctx.enter_context(tc.tile_pool(name="stat", bufs=4))
-        scrap_pool = ctx.enter_context(tc.tile_pool(name="scrap", bufs=4))
-        y_pool = ctx.enter_context(tc.tile_pool(name="y", bufs=2))
-        soft_pool = ctx.enter_context(tc.tile_pool(name="soft", bufs=6))
+        scrap_pool = ctx.enter_context(tc.tile_pool(name="scrap", bufs=2))
+        y_pool = ctx.enter_context(tc.tile_pool(name="y", bufs=3))
+        yq_pool = ctx.enter_context(tc.tile_pool(name="yq", bufs=4))
+        soft_pool = ctx.enter_context(tc.tile_pool(name="soft", bufs=4))
         psum = ctx.enter_context(tc.psum_pool(name="psum", bufs=2))
 
-        x_loaded, x_quantised, w_loaded, w_quantised = {}, {}, {}, {}
-        summed, rstds, normeds, rectified, y_quantised = {}, {}, {}, {}, {}
+        x_loaded, x_grouped, x_quantised = {}, {}, {}
+        w_loaded, w_grouped, w_quantised = {}, {}, {}
+        projected, summed, totals, square_sums, stats, normed = {}, {}, {}, {}, {}, {}
+        turned, planes, y_grouped, y_quantised = {}, {}, {}, {}
         sims, logits, exponentials = {}, {}, {}
 
-        def load_features(group):
+        def load_features(tile):
+            group, r = divmod(tile, TILES)
             batch, stream = divmod(group, STREAMS)
-            x_in = x_pool.tile([P, TILES * K], BF16, tag="x_in")
+            x_in = x_pool.tile([P, K], BF16, tag="x_in")
             nc.sync.dma_start(
-                out=x_in[:].rearrange("p (r k) -> p r k", r=TILES),
-                in_=features[stream][batch].rearrange("(r p) k -> p r k", p=P),
+                out=x_in[:], in_=features[stream][batch, r * P : (r + 1) * P, :]
             )
-            x_loaded[group] = x_in
+            x_loaded[tile] = x_in
 
-        def load_weight(stream):
-            w_raw = setup.tile([P, PASSES * PACK * D], BF16, tag="w_raw")
+        def load_weight(stream, g):
+            w_raw = setup.tile([P, PACK * D], BF16, tag="w_raw")
             nc.sync.dma_start(
-                out=w_raw[:].rearrange("q (a c) -> q a c", c=2 * D),
-                in_=weights[stream].rearrange("(a q e) c -> q a (e c)", q=P, e=2),
+                out=w_raw[:].rearrange("q (u c) -> q u c", c=2 * D),
+                in_=weights[stream][g * K_PASS : (g + 1) * K_PASS, :].rearrange(
+                    "(u q e) c -> q u (e c)", q=P, e=2
+                ),
             )
-            w_loaded[stream] = w_raw
-
-        bias_rows = []
-        for stream in range(STREAMS):
-            load_features(stream)
-            load_weight(stream)
-            bias_row = const.tile([P, D], BF16, name="bias_row%d" % stream)
-            nc.sync.dma_start(out=bias_row[:], in_=biases[stream].partition_broadcast(P))
-            bias_rows.append(bias_row)
-        gain_rows = const.tile([P, P], BF16)
-        nc.vector.memset(gain_rows[:], 0.0)
-        for j, vector in enumerate([vg, vbeta, lg, lbeta]):
-            nc.sync.dma_start(
-                out=gain_rows[PACK * j : PACK * (j + 1), :],
-                in_=vector.rearrange("(t c) -> t c", t=PACK),
-            )
-        claw_sb = const.tile([P, D * D // P], BF16)
-        nc.sync.dma_start(out=claw_sb[:], in_=claw.rearrange("(p a) c -> p (a c)", p=P))
+            w_loaded[(stream, g)] = w_raw
 
         ident = const.tile([P, P], F32)
         make_identity(nc, ident[:])
+        ones = const.tile([P, P], BF16)
+        nc.gpsimd.memset(ones[:], 1.0)
         neg_half = const.tile([P, TILES], F32)
-        nc.vector.memset(neg_half[:], -0.5)
+        nc.gpsimd.memset(neg_half[:], -0.5)
+        neg_one = const.tile([P, 1], F32)
+        nc.gpsimd.memset(neg_one[:], -1.0)
+        bias_pad = const.tile([P, STREAMS * D], BF16)
+        nc.vector.memset(bias_pad[:], 0.0)
+        gain_rows = const.tile([P, P], BF16)
+        nc.vector.memset(gain_rows[:], 0.0)
+        bias_rows = const.tile([P, STREAMS * D], F32)
         gains = const.tile([P, 4 * PACK], F32)
         neg_scale = const.tile([P, 1], F32)
+        claw_sb = const.tile([P, D * D // P], BF16)
+
+        def load_vectors():
+            for stream in range(STREAMS):
+                nc.sync.dma_start(
+                    out=bias_pad[0:1, stream * D : (stream + 1) * D],
+                    in_=biases[stream].rearrange("(o c) -> o c", o=1),
+                )
+            for j, vector in enumerate([lg, lbeta, vg, vbeta]):
+                nc.sync.dma_start(
+                    out=gain_rows[PACK * j : PACK * (j + 1), :],
+                    in_=vector.rearrange("(t c) -> t c", t=PACK),
+                )
+
+        def spread_biases():
+            for stream in range(STREAMS):
+                cols = slice(stream * D, (stream + 1) * D)
+                spread = psum.tile([P, D], F32, tag="sim")
+                nc.tensor.matmul(
+                    out=spread[:], lhsT=ones[:], rhs=bias_pad[:, cols], start=True, stop=True
+                )
+                nc.scalar.copy(out=bias_rows[:, cols], in_=spread[:])
 
         def prepare_gains():
             gain_rows_f32 = const.tile([P, P], F32)
@@ -101,15 +139,19 @@ def tile_clawmatrix_pa_t_kernel(
             nc.vector.tensor_copy(out=gains[:], in_=gains_ps[:, 0 : 4 * PACK])
 
         def prepare_scale():
-            partial = const.tile([P, 1], F32)
-            nc.vector.tensor_reduce(out=partial[:], in_=claw_sb[:], axis=AXIS_X, op=ALU.add)
-            repeated = const.tile([P, P], F32)
-            nc.vector.tensor_copy(out=repeated[:], in_=partial[:].to_broadcast([P, P]))
-            partials_ps = psum.tile([P, P], F32, tag="yt")
-            nc.tensor.transpose(out=partials_ps[:], in_=repeated[:], identity=ident[:])
+            columns = psum.tile([P, D], F32, tag="sim")
+            chunks = D // P
+            for a in range(chunks):
+                nc.tensor.matmul(
+                    out=columns[:],
+                    lhsT=ones[:],
+                    rhs=claw_sb[:, a * D : (a + 1) * D],
+                    start=(a == 0),
+                    stop=(a == chunks - 1),
+                )
             claw_sum = const.tile([P, 1], F32)
-            nc.vector.tensor_reduce(out=claw_sum[:], in_=partials_ps[:], axis=AXIS_X, op=ALU.add)
-            nc.vector.tensor_scalar(
+            nc.vector.tensor_reduce(out=claw_sum[:], in_=columns[:], axis=AXIS_X, op=ALU.add)
+            nc.gpsimd.tensor_scalar(
                 out=neg_scale[:],
                 in0=claw_sum[:],
                 scalar1=-1.0 / (D * D * TEMPERATURE),
@@ -117,164 +159,201 @@ def tile_clawmatrix_pa_t_kernel(
                 op0=ALU.mult,
             )
 
-        def quantise_weight(stream):
-            codes = const.tile([P, PASSES * D], U32, name="w_codes%d" % stream, align_bytes=64)
-            scales = const.tile([P, PASSES * D], U8, name="w_scales%d" % stream, align_bytes=64)
-            for g in range(PASSES):
-                w_grouped = setup.tile([P, D * PACK], BF16, tag="w_grouped", align_bytes=64)
-                nc.vector.tensor_copy(
-                    out=w_grouped[:].rearrange("p (c i t) -> p c t i", i=4, t=PACK),
-                    in_=w_loaded[stream][:, g * PACK * D : (g + 1) * PACK * D].rearrange(
-                        "p (t c i) -> p c t i", t=PACK, i=4
-                    ),
-                )
-                nc.vector.quantize_mx(
-                    out=codes[:, g * D : (g + 1) * D].bitcast(FP8X4),
-                    scales=scales[:, g * D : (g + 1) * D],
-                    in_=w_grouped[:],
-                )
-            w_quantised[stream] = (codes, scales)
-
-        def transpose_features(group):
-            x_words = x_loaded[group][:].bitcast(F32)
-            halves = []
-            for half in range(2):
-                x_grouped = xq_pool.tile(
-                    [P, 2 * PASSES * P * PACK], BF16, tag="x_grouped", align_bytes=64
-                )
-                x_grouped_words = x_grouped[:].bitcast(F32)
-                for i in range(2):
-                    r = 2 * half + i
-                    xt = psum.tile([P, WORDS], F32, tag="xt")
-                    for j in range(WORDS // P):
-                        nc.tensor.transpose(
-                            out=xt[:, j * P : (j + 1) * P],
-                            in_=x_words[:, r * WORDS + j * P : r * WORDS + (j + 1) * P],
-                            identity=ident[:],
-                        )
-                    nc.scalar.copy(
-                        out=x_grouped_words[:, i * WORDS : (i + 1) * WORDS].rearrange(
-                            "p (g c u) -> p g c u", g=PASSES, u=2
-                        ),
-                        in_=xt[:].rearrange("p (g u c) -> p g c u", g=PASSES, u=2),
-                    )
-                codes = xq_pool.tile([P, 2 * PASSES * P], U32, tag="x_codes", align_bytes=64)
-                scales = xq_pool.tile([P, 2 * PASSES * P], U8, tag="x_scales", align_bytes=64)
-                nc.vector.quantize_mx(
-                    out=codes[:].bitcast(FP8X4), scales=scales[:], in_=x_grouped[:]
-                )
-                halves.append((codes, scales))
-            x_quantised[group] = halves
-
-        def project(group):
-            stream = group % STREAMS
-            w_codes, w_scales = w_quantised[stream]
-            z = z_pool.tile([P, TILES, D], F32, tag="z")
-            sums = stat_pool.tile([P, TILES], F32, tag="sums")
-            for r in range(TILES):
-                codes, scales = x_quantised[group][r // 2]
-                h = psum.tile([P, D], F32, tag="h")
-                for g in range(PASSES):
-                    cols = slice(((r % 2) * PASSES + g) * P, ((r % 2) * PASSES + g + 1) * P)
-                    nc.tensor.matmul_mx(
-                        out=h[:],
-                        lhsT=codes[:, cols].bitcast(FP8X4),
-                        lhsT_scale=scales[:, cols],
-                        rhs=w_codes[:, g * D : (g + 1) * D].bitcast(FP8X4),
-                        rhs_scale=w_scales[:, g * D : (g + 1) * D],
-                        start=(g == 0),
-                        stop=(g == PASSES - 1),
-                    )
-                nc.vector.scalar_tensor_tensor(
-                    out=z[:, r, :],
-                    in0=h[:],
-                    scalar=1.0,
-                    in1=bias_rows[stream][:],
-                    op0=ALU.mult,
-                    op1=ALU.add,
-                    accum_out=sums[:, r : r + 1],
-                )
-            neg_mean = stat_pool.tile([P, TILES], F32, tag="neg_mean")
-            nc.vector.tensor_scalar(
-                out=neg_mean[:], in0=sums[:], scalar1=-1.0 / D, scalar2=None, op0=ALU.mult
+        def group_weight(stream, g, part, copy):
+            if part == 0:
+                wg = setup.tile([P, D * PACK], BF16, tag="w_grouped", align_bytes=64)
+                w_grouped[(stream, g)] = wg
+            width = D // W_PARTS
+            raw = w_loaded[(stream, g)][:].rearrange("p (t c) -> p t c", t=PACK)[
+                :, :, part * width : (part + 1) * width
+            ]
+            copy(
+                out=w_grouped[(stream, g)][
+                    :, part * width * PACK : (part + 1) * width * PACK
+                ].rearrange("p (c i t) -> p c t i", i=4, t=PACK),
+                in_=raw.rearrange("p t (c i) -> p c t i", i=4),
             )
-            summed[group] = (z, neg_mean)
 
-        def variance(group):
-            z, neg_mean = summed[group]
-            square_sums = stat_pool.tile([P, TILES], F32, tag="square_sums")
-            for r in range(TILES):
-                squares = scrap_pool.tile([P, D], BF16, tag="squares")
-                nc.scalar.activation(
-                    out=squares[:],
-                    in_=z[:, r, :],
-                    func=ACT.Square,
-                    bias=neg_mean[:, r : r + 1],
-                    scale=1.0,
-                    accum_out=square_sums[:, r : r + 1],
+        def quantise_weight(stream, g):
+            if g == 0:
+                w_codes = const.tile(
+                    [P, PASSES * D], U32, name="w_codes%d" % stream, align_bytes=64
                 )
+                w_scales = const.tile(
+                    [P, PASSES * D], U8, name="w_scales%d" % stream, align_bytes=64
+                )
+                w_quantised[stream] = (w_codes, w_scales)
+            codes, scales = w_quantised[stream]
+            nc.vector.quantize_mx(
+                out=codes[:, g * D : (g + 1) * D].bitcast(FP8X4),
+                scales=scales[:, g * D : (g + 1) * D],
+                in_=w_grouped[(stream, g)][:],
+            )
+
+        def transpose_features(tile):
+            x_words = x_loaded[tile][:].bitcast(F32)
+            xt = psum.tile([P, WORDS], F32, tag="xt")
+            for j in range(WORDS // P):
+                nc.tensor.transpose(
+                    out=xt[:, j * P : (j + 1) * P],
+                    in_=x_words[:, j * P : (j + 1) * P],
+                    identity=ident[:],
+                )
+            x_grouped[tile] = xt
+
+        def group_features(tile):
+            xt = x_grouped[tile]
+            xg = xq_pool.tile([P, K], BF16, tag="x_grouped", align_bytes=64)
+            nc.scalar.copy(
+                out=xg[:].bitcast(F32).rearrange("p (g c u) -> p g c u", g=PASSES, u=2),
+                in_=xt[:].rearrange("p (g u c) -> p g c u", g=PASSES, u=2),
+            )
+            x_grouped[tile] = xg
+
+        def quantise_features(tile):
+            codes = xq_pool.tile([P, PASSES * P], U32, tag="x_codes", align_bytes=64)
+            scales = xq_pool.tile([P, PASSES * P], U8, tag="x_scales", align_bytes=64)
+            nc.vector.quantize_mx(
+                out=codes[:].bitcast(FP8X4), scales=scales[:], in_=x_grouped[tile][:]
+            )
+            x_quantised[tile] = (codes, scales)
+
+        def project(tile):
+            stream = (tile // TILES) % STREAMS
+            w_codes, w_scales = w_quantised[stream]
+            codes, scales = x_quantised[tile]
+            h = psum.tile([P, D], F32, tag="h")
+            for g in range(PASSES):
+                nc.tensor.matmul_mx(
+                    out=h[:],
+                    lhsT=codes[:, g * P : (g + 1) * P].bitcast(FP8X4),
+                    lhsT_scale=scales[:, g * P : (g + 1) * P],
+                    rhs=w_codes[:, g * D : (g + 1) * D].bitcast(FP8X4),
+                    rhs_scale=w_scales[:, g * D : (g + 1) * D],
+                    start=(g == 0),
+                    stop=(g == PASSES - 1),
+                )
+            projected[tile] = h
+
+        def add_bias(tile):
+            stream = (tile // TILES) % STREAMS
+            group, r = divmod(tile, TILES)
+            if r == 0:
+                group_totals = stat_pool.tile([P, TILES], F32, tag="totals")
+                totals[group] = group_totals
+            z = z_pool.tile([P, D], F32, tag="z")
+            nc.vector.scalar_tensor_tensor(
+                out=z[:],
+                in0=projected[tile][:],
+                scalar=1.0,
+                in1=bias_rows[:, stream * D : (stream + 1) * D],
+                op0=ALU.mult,
+                op1=ALU.add,
+                accum_out=totals[group][:, r : r + 1],
+            )
+            summed[tile] = z
+
+        def square(tile):
+            group, r = divmod(tile, TILES)
+            if r == 0:
+                group_squares = stat_pool.tile([P, TILES], F32, tag="square_sums")
+                square_sums[group] = group_squares
+            squares = scrap_pool.tile([P, D], BF16, tag="squares")
+            nc.scalar.activation(
+                out=squares[:],
+                in_=summed[tile][:],
+                func=ACT.Square,
+                bias=totals[group][:, r : r + 1],
+                scale=-1.0 * D,
+                accum_out=square_sums[group][:, r : r + 1],
+            )
+
+        def statistics(group):
+            neg_mean = stat_pool.tile([P, TILES], F32, tag="neg_mean")
+            nc.gpsimd.tensor_scalar(
+                out=neg_mean[:],
+                in0=totals[group][:],
+                scalar1=-1.0 / D,
+                scalar2=None,
+                op0=ALU.mult,
+            )
             var_eps = stat_pool.tile([P, TILES], F32, tag="var_eps")
             nc.gpsimd.tensor_scalar(
                 out=var_eps[:],
-                in0=square_sums[:],
-                scalar1=1.0 / D,
+                in0=square_sums[group][:],
+                scalar1=1.0 / (D * D * D),
                 scalar2=EPS,
                 op0=ALU.mult,
                 op1=ALU.add,
             )
             rstd = stat_pool.tile([P, TILES], F32, tag="rstd")
             nc.gpsimd.tensor_tensor(out=rstd[:], in0=var_eps[:], in1=neg_half[:], op=ALU.pow)
-            rstds[group] = rstd
+            stats[group] = (neg_mean, rstd)
 
-        def normalise(group):
-            z, neg_mean = summed[group]
-            normed = y_pool.tile([P, TILES, D], F32, tag="normed")
-            for r in range(TILES):
-                nc.vector.tensor_scalar(
-                    out=normed[:, r, :],
-                    in0=z[:, r, :],
-                    scalar1=neg_mean[:, r : r + 1],
-                    scalar2=rstds[group][:, r : r + 1],
-                    op0=ALU.add,
-                    op1=ALU.mult,
-                )
-            normeds[group] = normed
-
-        def rectify(group):
-            first = 2 * PACK * (group % STREAMS)
-            planes = y_pool.tile([P, PACK, S], BF16, tag="planes")
-            for t in range(PACK):
-                yt = psum.tile([P, S], F32, tag="yt")
-                for r in range(TILES):
-                    nc.tensor.transpose(
-                        out=yt[:, r * P : (r + 1) * P],
-                        in_=normeds[group][:, r, t * P : (t + 1) * P],
-                        identity=ident[:],
-                    )
-                nc.scalar.activation(
-                    out=planes[:, t, :],
-                    in_=yt[:],
-                    func=ACT.Relu,
-                    bias=gains[:, first + PACK + t : first + PACK + t + 1],
-                    scale=gains[:, first + t : first + t + 1],
-                )
-            rectified[group] = planes
-
-        def quantise_rectified(group):
-            y_grouped = y_pool.tile([P, S * PACK], BF16, tag="y_grouped", align_bytes=64)
-            nc.vector.tensor_copy(
-                out=y_grouped[:].rearrange("p (c i t) -> p c t i", i=4, t=PACK),
-                in_=rectified[group][:].rearrange("p t (c i) -> p c t i", i=4),
+        def normalise(tile):
+            group, r = divmod(tile, TILES)
+            neg_mean, rstd = stats[group]
+            n = n_pool.tile([P, D], F32, tag="normed")
+            nc.vector.tensor_scalar(
+                out=n[:],
+                in0=summed[tile][:],
+                scalar1=neg_mean[:, r : r + 1],
+                scalar2=rstd[:, r : r + 1],
+                op0=ALU.add,
+                op1=ALU.mult,
             )
-            stream = group % STREAMS
-            codes = y_pool.tile([P, S], U32, tag="y_codes%d" % stream, align_bytes=64)
-            scales = y_pool.tile([P, S], U8, tag="y_scales%d" % stream, align_bytes=64)
-            nc.vector.quantize_mx(out=codes[:].bitcast(FP8X4), scales=scales[:], in_=y_grouped[:])
-            y_quantised[group] = (codes, scales)
+            normed[tile] = n
+
+        def transpose_plane(group, t):
+            yt = psum.tile([P, S], F32, tag="yt")
+            for r in range(TILES):
+                nc.tensor.transpose(
+                    out=yt[:, r * P : (r + 1) * P],
+                    in_=normed[group * TILES + r][:, t * P : (t + 1) * P],
+                    identity=ident[:],
+                )
+            turned[(group, t)] = yt
+
+        def rectify_plane(group, t):
+            first = 2 * PACK * (group % STREAMS)
+            if t == 0:
+                y_planes = y_pool.tile([P, PACK, S], BF16, tag="planes")
+                planes[group] = y_planes
+            nc.scalar.activation(
+                out=planes[group][:, t, :],
+                in_=turned[(group, t)][:],
+                func=ACT.Relu,
+                bias=gains[:, first + PACK + t : first + PACK + t + 1],
+                scale=gains[:, first + t : first + t + 1],
+            )
+
+        def regroup(tile):
+            group, r = divmod(tile, TILES)
+            yg = y_pool.tile([P, P * PACK], BF16, tag="y_grouped", align_bytes=64)
+            nc.vector.tensor_copy(
+                out=yg[:].rearrange("p (c i t) -> p c t i", i=4, t=PACK),
+                in_=planes[group][:, :, r * P : (r + 1) * P].rearrange(
+                    "p t (c i) -> p c t i", i=4
+                ),
+            )
+            y_grouped[tile] = yg
+
+        def quantise_rectified(tile):
+            group, r = divmod(tile, TILES)
+            if r == 0:
+                y_codes = yq_pool.tile([P, S], U32, tag="y_codes", align_bytes=64)
+                y_scales = yq_pool.tile([P, S], U8, tag="y_scales", align_bytes=64)
+                y_quantised[group] = (y_codes, y_scales)
+            codes, scales = y_quantised[group]
+            nc.vector.quantize_mx(
+                out=codes[:, r * P : (r + 1) * P].bitcast(FP8X4),
+                scales=scales[:, r * P : (r + 1) * P],
+                in_=y_grouped[tile][:],
+            )
 
         def similarity(batch, r):
-            v_codes, v_scales = y_quantised[STREAMS * batch]
-            l_codes, l_scales = y_quantised[STREAMS * batch + 1]
+            v_codes, v_scales = y_quantised[STREAMS * batch + VISION]
+            l_codes, l_scales = y_quantised[STREAMS * batch + LANGUAGE]
             sim = psum.tile([P, S], F32, tag="sim")
             nc.tensor.matmul_mx(
                 out=sim[:],
@@ -313,53 +392,91 @@ def tile_clawmatrix_pa_t_kernel(
                 scale=-1.0,
                 accum_out=row_sum[:],
             )
-            exponentials[(batch, r)] = (probs, row_sum)
+            inverse = soft_pool.tile([P, 1], F32, tag="inverse")
+            nc.gpsimd.tensor_tensor(out=inverse[:], in0=row_sum[:], in1=neg_one[:], op=ALU.pow)
+            exponentials[(batch, r)] = (probs, inverse)
 
         def store_probabilities(batch, r):
-            probs, row_sum = exponentials[(batch, r)]
-            inverse = soft_pool.tile([P, 1], F32, tag="inverse")
-            nc.vector.reciprocal(out=inverse[:], in_=row_sum[:])
+            probs, inverse = exponentials[(batch, r)]
             nc.vector.tensor_scalar(
                 out=probs[:], in0=probs[:], scalar1=inverse[:], scalar2=None, op0=ALU.mult
             )
             nc.sync.dma_start(out=out[batch, r * P : (r + 1) * P, :], in_=probs[:])
 
-        def tile_pair(n):
-            if not 0 <= n < GROUPS:
-                return []
-            return [(n // 2, 2 * (n % 2)), (n // 2, 2 * (n % 2) + 1)]
+        def tile_at(step):
+            return [step] if 0 <= step < ALL_TILES else []
 
-        def in_range(group):
-            return 0 <= group < GROUPS
+        def plane_at(step):
+            return [divmod(step, TILES)] if 0 <= step < ALL_TILES else []
 
-        for step in range(GROUPS + 5):
-            if in_range(step + 2):
-                load_features(step + 2)
-            if in_range(step - 3):
-                quantise_rectified(step - 3)
-            if in_range(step - 2):
-                normalise(step - 2)
-            if step == 0:
-                quantise_weight(0)
-            if in_range(step):
-                transpose_features(step)
-            for batch, r in tile_pair(step - 5):
-                exponentiate(batch, r)
-            for batch, r in tile_pair(step - 4):
-                similarity(batch, r)
-            if in_range(step):
-                project(step)
-            for batch, r in tile_pair(step - 4):
-                scale_logits(batch, r)
-            for batch, r in tile_pair(step - 5):
-                store_probabilities(batch, r)
-            if step == 0:
-                quantise_weight(1)
-            if in_range(step - 1):
-                variance(step - 1)
-            if in_range(step - 2):
-                rectify(step - 2)
-            if step == 0:
-                prepare_gains()
-            if step == 1:
-                prepare_scale()
+        def sim_at(step):
+            batch, rest = divmod(step - TILES, STREAMS * TILES)
+            return [(batch, rest // 2)] if 0 <= batch < B and rest % 2 == 0 else []
+
+        with tc.manual_schedule():
+            load_weight(0, 0)
+            load_vectors()
+            load_weight(0, 1)
+            for tile in range(TILES):
+                load_features(tile)
+            for g in range(PASSES):
+                load_weight(1, g)
+            for tile in range(TILES, LOAD_AHEAD):
+                load_features(tile)
+            nc.sync.dma_start(out=claw_sb[:], in_=claw.rearrange("(p a) c -> p (a c)", p=P))
+
+            for step in range(ALL_TILES + LAG_STORE + TILES):
+                for tile in tile_at(step):
+                    transpose_features(tile)
+                for group, t in plane_at(step - LAG_TURN):
+                    transpose_plane(group, t)
+                if step == 0:
+                    for part in range(W_PARTS):
+                        group_weight(0, 0, part, nc.vector.tensor_copy)
+                    for part in range(W_PARTS // 2):
+                        group_weight(0, 1, part, nc.vector.tensor_copy)
+                    for part in range(W_PARTS // 2, W_PARTS):
+                        group_weight(0, 1, part, nc.scalar.copy)
+                    quantise_weight(0, 0)
+                    quantise_weight(0, 1)
+                if step in (4, 6):
+                    quantise_weight(1, (step - 4) // 2)
+                if step == LAG_TURN - 2:
+                    prepare_gains()
+                for tile in tile_at(step - LAG_QUANT):
+                    quantise_features(tile)
+                for tile in tile_at(step - LAG_NORM):
+                    normalise(tile)
+                for tile in tile_at(step - LAG_REGROUP):
+                    regroup(tile)
+                for batch, r in sim_at(step - LAG_STORE):
+                    store_probabilities(batch, r)
+                for tile in tile_at(step - LAG_YQUANT):
+                    quantise_rectified(tile)
+                for tile in tile_at(step - LAG_PROJECT):
+                    project(tile)
+                for batch, r in sim_at(step - LAG_SIM):
+                    similarity(batch, r)
+                if step == LAG_SIM - 2:
+                    prepare_scale()
+                for tile in tile_at(step - LAG_SQUARE):
+                    square(tile)
+                    if tile % TILES == TILES - 1:
+                        statistics(tile // TILES)
+                for group, t in plane_at(step - LAG_RELU):
+                    rectify_plane(group, t)
+                for batch, r in sim_at(step - LAG_EXP):
+                    exponentiate(batch, r)
+                for tile in tile_at(step):
+                    group_features(tile)
+                if step == 1:
+                    spread_biases()
+                if 2 <= step < 2 + TILES:
+                    for piece in (2 * step - 4, 2 * step - 3):
+                        group_weight(1, piece // W_PARTS, piece % W_PARTS, nc.scalar.copy)
+                for tile in tile_at(step - LAG_SUM):
+                    add_bias(tile)
+                for batch, r in sim_at(step - LAG_LOGITS):
+                    scale_logits(batch, r)
+                for tile in tile_at(step + LOAD_AHEAD):
+                    load_features(tile)

@@ -32,16 +32,16 @@ FLOPS = 2 * STREAMS * B * S * K * D + 2 * B * S * S * D
 LAG_QUANT = 2
 LAG_PROJECT = 2
 LAG_SUM = 3
-LAG_SQUARE = 5
-LAG_NORM = 10
-LAG_TURN = 14
-LAG_RELU = 14
-LAG_REGROUP = 19
-LAG_YQUANT = 20
-LAG_SIM = 21
-LAG_LOGITS = 22
-LAG_EXP = 23
-LAG_STORE = 25
+LAG_SQUARE = 4
+LAG_NORM = 9
+LAG_TURN = 13
+LAG_RELU = 13
+LAG_REGROUP = 18
+LAG_YQUANT = 19
+LAG_SIM = 20
+LAG_LOGITS = 21
+LAG_EXP = 22
+LAG_STORE = 24
 LOAD_AHEAD = 8
 W_PARTS = 4
 
@@ -133,10 +133,12 @@ def tile_clawmatrix_pa_t_kernel(
 
         def prepare_gains():
             gain_rows_f32 = const.tile([P, P], F32)
-            nc.vector.tensor_copy(out=gain_rows_f32[:], in_=gain_rows[:])
+            nc.scalar.copy(out=gain_rows_f32[:], in_=gain_rows[:])
             gains_ps = psum.tile([P, P], F32, tag="yt")
             nc.tensor.transpose(out=gains_ps[:], in_=gain_rows_f32[:], identity=ident[:])
-            nc.vector.tensor_copy(out=gains[:], in_=gains_ps[:, 0 : 4 * PACK])
+            nc.scalar.copy(out=gains[:], in_=gains_ps[:, 0 : 4 * PACK])
+
+        claw_columns = []
 
         def prepare_scale():
             columns = psum.tile([P, D], F32, tag="sim")
@@ -149,8 +151,11 @@ def tile_clawmatrix_pa_t_kernel(
                     start=(a == 0),
                     stop=(a == chunks - 1),
                 )
+            claw_columns.append(columns)
+
+        def finish_scale():
             claw_sum = const.tile([P, 1], F32)
-            nc.vector.tensor_reduce(out=claw_sum[:], in_=columns[:], axis=AXIS_X, op=ALU.add)
+            nc.vector.tensor_reduce(out=claw_sum[:], in_=claw_columns[0][:], axis=AXIS_X, op=ALU.add)
             nc.gpsimd.tensor_scalar(
                 out=neg_scale[:],
                 in0=claw_sum[:],
@@ -441,8 +446,6 @@ def tile_clawmatrix_pa_t_kernel(
                     quantise_weight(0, 1)
                 if step in (4, 6):
                     quantise_weight(1, (step - 4) // 2)
-                if step == LAG_TURN - 2:
-                    prepare_gains()
                 for tile in tile_at(step - LAG_QUANT):
                     quantise_features(tile)
                 for tile in tile_at(step - LAG_NORM):
@@ -457,8 +460,10 @@ def tile_clawmatrix_pa_t_kernel(
                     project(tile)
                 for batch, r in sim_at(step - LAG_SIM):
                     similarity(batch, r)
-                if step == LAG_SIM - 2:
+                if step == LAG_TURN - 4:
                     prepare_scale()
+                if step == LAG_TURN - 2:
+                    finish_scale()
                 for tile in tile_at(step - LAG_SQUARE):
                     square(tile)
                     if tile % TILES == TILES - 1:
@@ -471,9 +476,10 @@ def tile_clawmatrix_pa_t_kernel(
                     group_features(tile)
                 if step == 1:
                     spread_biases()
+                    prepare_gains()
                 if 2 <= step < 2 + TILES:
                     for piece in (2 * step - 4, 2 * step - 3):
-                        group_weight(1, piece // W_PARTS, piece % W_PARTS, nc.scalar.copy)
+                        group_weight(1, piece // W_PARTS, piece % W_PARTS, nc.vector.tensor_copy)
                 for tile in tile_at(step - LAG_SUM):
                     add_bias(tile)
                 for batch, r in sim_at(step - LAG_LOGITS):

@@ -74,6 +74,11 @@ def tile_clawmatrix_pa_t_kernel(
         turned, planes, y_grouped, y_quantised = {}, {}, {}, {}
         sims, logits, exponentials = {}, {}, {}
 
+        def regroup_on_scalar(tile):
+            if tile + LAG_REGROUP >= ALL_TILES:
+                return tile % 2 == 1
+            return tile % 8 == 7
+
         def load_features(tile):
             group, r = divmod(tile, TILES)
             batch, stream = divmod(group, STREAMS)
@@ -335,7 +340,8 @@ def tile_clawmatrix_pa_t_kernel(
         def regroup(tile):
             group, r = divmod(tile, TILES)
             yg = y_pool.tile([P, P * PACK], BF16, tag="y_grouped", align_bytes=64)
-            nc.vector.tensor_copy(
+            copy = nc.scalar.copy if regroup_on_scalar(tile) else nc.vector.tensor_copy
+            copy(
                 out=yg[:].rearrange("p (c i t) -> p c t i", i=4, t=PACK),
                 in_=planes[group][:, :, r * P : (r + 1) * P].rearrange(
                     "p t (c i) -> p c t i", i=4
@@ -431,6 +437,8 @@ def tile_clawmatrix_pa_t_kernel(
             nc.sync.dma_start(out=claw_sb[:], in_=claw.rearrange("(p a) c -> p (a c)", p=P))
 
             for step in range(ALL_TILES + LAG_STORE + TILES):
+                if step == 0:
+                    spread_biases()
                 for tile in tile_at(step):
                     transpose_features(tile)
                 for group, t in plane_at(step - LAG_TURN):
@@ -474,8 +482,7 @@ def tile_clawmatrix_pa_t_kernel(
                     exponentiate(batch, r)
                 for tile in tile_at(step):
                     group_features(tile)
-                if step == 1:
-                    spread_biases()
+                if step == 5:
                     prepare_gains()
                 if 2 <= step < 2 + TILES:
                     for piece in (2 * step - 4, 2 * step - 3):

@@ -57,15 +57,17 @@ def tile_clawmatrix_pa_t_kernel(
     with ExitStack() as ctx:
         const = ctx.enter_context(tc.tile_pool(name="const", bufs=1))
         setup = ctx.enter_context(tc.tile_pool(name="setup", bufs=STREAMS * PASSES))
-        x_pool = ctx.enter_context(tc.tile_pool(name="x", bufs=16))
+        x_pool = ctx.enter_context(tc.tile_pool(name="x", bufs=3))
+        x0_pool = ctx.enter_context(tc.tile_pool(name="x0", bufs=TILES))
         xq_pool = ctx.enter_context(tc.tile_pool(name="xq", bufs=6))
         z_pool = ctx.enter_context(tc.tile_pool(name="z", bufs=10))
-        n_pool = ctx.enter_context(tc.tile_pool(name="n", bufs=14))
+        n_pool = ctx.enter_context(tc.tile_pool(name="n", bufs=12))
         stat_pool = ctx.enter_context(tc.tile_pool(name="stat", bufs=4))
-        scrap_pool = ctx.enter_context(tc.tile_pool(name="scrap", bufs=2))
+        scrap_pool = ctx.enter_context(tc.tile_pool(name="scrap", bufs=8))
         y_pool = ctx.enter_context(tc.tile_pool(name="y", bufs=3))
         yq_pool = ctx.enter_context(tc.tile_pool(name="yq", bufs=4))
         soft_pool = ctx.enter_context(tc.tile_pool(name="soft", bufs=4))
+        prob_pool = ctx.enter_context(tc.tile_pool(name="prob", bufs=16))
         psum = ctx.enter_context(tc.psum_pool(name="psum", bufs=2))
 
         x_loaded, x_grouped, x_quantised = {}, {}, {}
@@ -79,14 +81,19 @@ def tile_clawmatrix_pa_t_kernel(
                 return tile % 2 == 1
             return tile % 8 == 7
 
-        def load_features(tile):
-            group, r = divmod(tile, TILES)
+        def load_features(first, count):
+            group, r = divmod(first, TILES)
             batch, stream = divmod(group, STREAMS)
-            x_in = x_pool.tile([P, K], BF16, tag="x_in")
+            pool = x0_pool if count == 1 else x_pool
+            x_in = pool.tile([P, count, K], BF16, tag="x_in%d" % count)
             nc.sync.dma_start(
-                out=x_in[:], in_=features[stream][batch, r * P : (r + 1) * P, :]
+                out=x_in[:],
+                in_=features[stream][batch, r * P : (r + count) * P, :].rearrange(
+                    "(i p) k -> p i k", p=P
+                ),
             )
-            x_loaded[tile] = x_in
+            for i in range(count):
+                x_loaded[first + i] = x_in[:, i, :]
 
         def load_weight(stream, g):
             w_raw = setup.tile([P, PACK * D], BF16, tag="w_raw")
@@ -201,7 +208,7 @@ def tile_clawmatrix_pa_t_kernel(
             )
 
         def transpose_features(tile):
-            x_words = x_loaded[tile][:].bitcast(F32)
+            x_words = x_loaded[tile].bitcast(F32)
             xt = psum.tile([P, WORDS], F32, tag="xt")
             for j in range(WORDS // P):
                 nc.tensor.transpose(
@@ -393,7 +400,7 @@ def tile_clawmatrix_pa_t_kernel(
 
         def exponentiate(batch, r):
             neg_logits, neg_max = logits[(batch, r)]
-            probs = soft_pool.tile([P, S], F32, tag="probs")
+            probs = prob_pool.tile([P, S], F32, tag="probs")
             row_sum = soft_pool.tile([P, 1], F32, tag="row_sum")
             nc.scalar.activation(
                 out=probs[:],
@@ -429,11 +436,11 @@ def tile_clawmatrix_pa_t_kernel(
             load_vectors()
             load_weight(0, 1)
             for tile in range(TILES):
-                load_features(tile)
+                load_features(tile, 1)
             for g in range(PASSES):
                 load_weight(1, g)
-            for tile in range(TILES, LOAD_AHEAD):
-                load_features(tile)
+            for first in range(TILES, LOAD_AHEAD, TILES):
+                load_features(first, TILES)
             nc.sync.dma_start(out=claw_sb[:], in_=claw.rearrange("(p a) c -> p (a c)", p=P))
 
             for step in range(ALL_TILES + LAG_STORE + TILES):
@@ -491,5 +498,6 @@ def tile_clawmatrix_pa_t_kernel(
                     add_bias(tile)
                 for batch, r in sim_at(step - LAG_LOGITS):
                     scale_logits(batch, r)
-                for tile in tile_at(step + LOAD_AHEAD):
-                    load_features(tile)
+                for first in tile_at(step + LOAD_AHEAD):
+                    if first % TILES == 0:
+                        load_features(first, TILES)

@@ -77,9 +77,7 @@ def tile_clawmatrix_pa_t_kernel(
         sims, logits, exponentials = {}, {}, {}
 
         def regroup_on_scalar(tile):
-            if tile + LAG_REGROUP >= ALL_TILES:
-                return tile % 2 == 1
-            return tile % 8 == 7
+            return tile + LAG_REGROUP >= ALL_TILES + TILES and tile % TILES == TILES - 1
 
         def load_features(first, count):
             group, r = divmod(first, TILES)

@@ -43,6 +43,7 @@ LAG_LOGITS = 21
 LAG_EXP = 22
 LAG_STORE = 24
 LOAD_AHEAD = 8
+PAIR = 2
 W_PARTS = 4
 
 
@@ -70,7 +71,7 @@ def tile_clawmatrix_pa_t_kernel(
         prob_pool = ctx.enter_context(tc.tile_pool(name="prob", bufs=16))
         psum = ctx.enter_context(tc.psum_pool(name="psum", bufs=2))
 
-        x_loaded, x_grouped, x_quantised = {}, {}, {}
+        x_loaded, x_turned, x_grouped, x_quantised = {}, {}, {}, {}
         w_loaded, w_grouped, w_quantised = {}, {}, {}
         projected, summed, totals, square_sums, stats, normed = {}, {}, {}, {}, {}, {}
         turned, planes, y_grouped, y_quantised = {}, {}, {}, {}
@@ -78,6 +79,10 @@ def tile_clawmatrix_pa_t_kernel(
 
         def regroup_on_scalar(tile):
             return tile + LAG_REGROUP >= ALL_TILES + TILES and tile % TILES == TILES - 1
+
+        def chunk_of(tile):
+            first = tile - tile % PAIR
+            return (tile, 1) if first + LAG_REGROUP >= ALL_TILES else (first, PAIR)
 
         def load_features(first, count):
             group, r = divmod(first, TILES)
@@ -214,14 +219,13 @@ def tile_clawmatrix_pa_t_kernel(
                     in_=x_words[:, j * P : (j + 1) * P],
                     identity=ident[:],
                 )
-            x_grouped[tile] = xt
+            x_turned[tile] = xt
 
         def group_features(tile):
-            xt = x_grouped[tile]
             xg = xq_pool.tile([P, K], BF16, tag="x_grouped", align_bytes=64)
             nc.scalar.copy(
                 out=xg[:].bitcast(F32).rearrange("p (g c u) -> p g c u", g=PASSES, u=2),
-                in_=xt[:].rearrange("p (g u c) -> p g c u", g=PASSES, u=2),
+                in_=x_turned[tile][:].rearrange("p (g u c) -> p g c u", g=PASSES, u=2),
             )
             x_grouped[tile] = xg
 
@@ -343,28 +347,34 @@ def tile_clawmatrix_pa_t_kernel(
             )
 
         def regroup(tile):
-            group, r = divmod(tile, TILES)
-            yg = y_pool.tile([P, P * PACK], BF16, tag="y_grouped", align_bytes=64)
+            first, count = chunk_of(tile)
+            if tile != first + count - 1:
+                return
+            group, r = divmod(first, TILES)
+            yg = y_pool.tile([P, PAIR * P * PACK], BF16, tag="y_grouped", align_bytes=64)
             copy = nc.scalar.copy if regroup_on_scalar(tile) else nc.vector.tensor_copy
             copy(
-                out=yg[:].rearrange("p (c i t) -> p c t i", i=4, t=PACK),
-                in_=planes[group][:, :, r * P : (r + 1) * P].rearrange(
+                out=yg[:, 0 : count * P * PACK].rearrange("p (c i t) -> p c t i", i=4, t=PACK),
+                in_=planes[group][:, :, r * P : (r + count) * P].rearrange(
                     "p t (c i) -> p c t i", i=4
                 ),
             )
-            y_grouped[tile] = yg
+            y_grouped[first] = yg
 
         def quantise_rectified(tile):
-            group, r = divmod(tile, TILES)
+            first, count = chunk_of(tile)
+            if tile != first + count - 1:
+                return
+            group, r = divmod(first, TILES)
             if r == 0:
                 y_codes = yq_pool.tile([P, S], U32, tag="y_codes", align_bytes=64)
                 y_scales = yq_pool.tile([P, S], U8, tag="y_scales", align_bytes=64)
                 y_quantised[group] = (y_codes, y_scales)
             codes, scales = y_quantised[group]
             nc.vector.quantize_mx(
-                out=codes[:, r * P : (r + 1) * P].bitcast(FP8X4),
-                scales=scales[:, r * P : (r + 1) * P],
-                in_=y_grouped[tile][:],
+                out=codes[:, r * P : (r + count) * P].bitcast(FP8X4),
+                scales=scales[:, r * P : (r + count) * P],
+                in_=y_grouped[first][:, 0 : count * P * PACK],
             )
 
         def similarity(batch, r):
@@ -481,12 +491,12 @@ def tile_clawmatrix_pa_t_kernel(
                     square(tile)
                     if tile % TILES == TILES - 1:
                         statistics(tile // TILES)
-                for group, t in plane_at(step - LAG_RELU):
-                    rectify_plane(group, t)
-                for batch, r in sim_at(step - LAG_EXP):
-                    exponentiate(batch, r)
                 for tile in tile_at(step):
                     group_features(tile)
+                for batch, r in sim_at(step - LAG_EXP):
+                    exponentiate(batch, r)
+                for group, t in plane_at(step - LAG_RELU):
+                    rectify_plane(group, t)
                 if step == 5:
                     prepare_gains()
                 if 2 <= step < 2 + TILES:

@@ -33,6 +33,7 @@ LAG_QUANT = 2
 LAG_PROJECT = 2
 LAG_SUM = 3
 LAG_SQUARE = 4
+LAG_STATS = 5
 LAG_NORM = 9
 LAG_TURN = 13
 LAG_RELU = 13
@@ -41,7 +42,8 @@ LAG_YQUANT = 19
 LAG_SIM = 20
 LAG_LOGITS = 21
 LAG_EXP = 22
-LAG_STORE = 24
+LAG_INVERT = 24
+LAG_STORE = 28
 LOAD_AHEAD = 8
 PAIR = 2
 W_PARTS = 4
@@ -73,9 +75,9 @@ def tile_clawmatrix_pa_t_kernel(
 
         x_loaded, x_turned, x_grouped, x_quantised = {}, {}, {}, {}
         w_loaded, w_grouped, w_quantised = {}, {}, {}
-        projected, summed, totals, square_sums, stats, normed = {}, {}, {}, {}, {}, {}
+        projected, summed, sums, stats, normed = {}, {}, {}, {}, {}
         turned, planes, y_grouped, y_quantised = {}, {}, {}, {}
-        sims, logits, exponentials = {}, {}, {}
+        sims, logits, exponentials, row_sums, inverses = {}, {}, {}, {}, {}
 
         def regroup_on_scalar(tile):
             return tile + LAG_REGROUP >= ALL_TILES + TILES and tile % TILES == TILES - 1
@@ -112,10 +114,11 @@ def tile_clawmatrix_pa_t_kernel(
         make_identity(nc, ident[:])
         ones = const.tile([P, P], BF16)
         nc.gpsimd.memset(ones[:], 1.0)
+        eps_row = const.tile([P, 2 * TILES], F32)
+        nc.vector.memset(eps_row[:, 0:TILES], 0.0)
+        nc.vector.memset(eps_row[:, TILES : 2 * TILES], D * D * EPS)
         neg_half = const.tile([P, TILES], F32)
         nc.gpsimd.memset(neg_half[:], -0.5)
-        neg_one = const.tile([P, 1], F32)
-        nc.gpsimd.memset(neg_one[:], -1.0)
         bias_pad = const.tile([P, STREAMS * D], BF16)
         nc.vector.memset(bias_pad[:], 0.0)
         gain_rows = const.tile([P, P], BF16)
@@ -151,7 +154,12 @@ def tile_clawmatrix_pa_t_kernel(
             nc.scalar.copy(out=gain_rows_f32[:], in_=gain_rows[:])
             gains_ps = psum.tile([P, P], F32, tag="yt")
             nc.tensor.transpose(out=gains_ps[:], in_=gain_rows_f32[:], identity=ident[:])
-            nc.scalar.copy(out=gains[:], in_=gains_ps[:, 0 : 4 * PACK])
+            used = gains_ps[:, 0 : 4 * PACK].rearrange("p (m j t) -> p m j t", m=STREAMS, j=2)
+            kept = gains[:].rearrange("p (m j t) -> p m j t", m=STREAMS, j=2)
+            nc.scalar.activation(
+                out=kept[:, :, 0, :], in_=used[:, :, 0, :], func=ACT.Copy, scale=1.0 * D
+            )
+            nc.scalar.copy(out=kept[:, :, 1, :], in_=used[:, :, 1, :])
 
         claw_columns = []
 
@@ -258,8 +266,8 @@ def tile_clawmatrix_pa_t_kernel(
             stream = (tile // TILES) % STREAMS
             group, r = divmod(tile, TILES)
             if r == 0:
-                group_totals = stat_pool.tile([P, TILES], F32, tag="totals")
-                totals[group] = group_totals
+                group_sums = stat_pool.tile([P, 2 * TILES], F32, tag="sums")
+                sums[group] = group_sums
             z = z_pool.tile([P, D], F32, tag="z")
             nc.vector.scalar_tensor_tensor(
                 out=z[:],
@@ -268,57 +276,48 @@ def tile_clawmatrix_pa_t_kernel(
                 in1=bias_rows[:, stream * D : (stream + 1) * D],
                 op0=ALU.mult,
                 op1=ALU.add,
-                accum_out=totals[group][:, r : r + 1],
+                accum_out=sums[group][:, r : r + 1],
             )
             summed[tile] = z
 
         def square(tile):
             group, r = divmod(tile, TILES)
-            if r == 0:
-                group_squares = stat_pool.tile([P, TILES], F32, tag="square_sums")
-                square_sums[group] = group_squares
             squares = scrap_pool.tile([P, D], BF16, tag="squares")
             nc.scalar.activation(
                 out=squares[:],
                 in_=summed[tile][:],
                 func=ACT.Square,
-                bias=totals[group][:, r : r + 1],
+                bias=sums[group][:, r : r + 1],
                 scale=-1.0 * D,
-                accum_out=square_sums[group][:, r : r + 1],
+                accum_out=sums[group][:, TILES + r : TILES + r + 1],
             )
 
         def statistics(group):
-            neg_mean = stat_pool.tile([P, TILES], F32, tag="neg_mean")
-            nc.gpsimd.tensor_scalar(
-                out=neg_mean[:],
-                in0=totals[group][:],
-                scalar1=-1.0 / D,
-                scalar2=None,
-                op0=ALU.mult,
-            )
-            var_eps = stat_pool.tile([P, TILES], F32, tag="var_eps")
-            nc.gpsimd.tensor_scalar(
-                out=var_eps[:],
-                in0=square_sums[group][:],
-                scalar1=1.0 / (D * D * D),
-                scalar2=EPS,
+            means = stat_pool.tile([P, 2 * TILES], F32, tag="means")
+            nc.vector.scalar_tensor_tensor(
+                out=means[:],
+                in0=sums[group][:],
+                scalar=1.0 / D,
+                in1=eps_row[:],
                 op0=ALU.mult,
                 op1=ALU.add,
             )
             rstd = stat_pool.tile([P, TILES], F32, tag="rstd")
-            nc.gpsimd.tensor_tensor(out=rstd[:], in0=var_eps[:], in1=neg_half[:], op=ALU.pow)
-            stats[group] = (neg_mean, rstd)
+            nc.gpsimd.tensor_tensor(
+                out=rstd[:], in0=means[:, TILES : 2 * TILES], in1=neg_half[:], op=ALU.pow
+            )
+            stats[group] = (means, rstd)
 
         def normalise(tile):
             group, r = divmod(tile, TILES)
-            neg_mean, rstd = stats[group]
+            means, rstd = stats[group]
             n = n_pool.tile([P, D], F32, tag="normed")
             nc.vector.tensor_scalar(
                 out=n[:],
                 in0=summed[tile][:],
-                scalar1=neg_mean[:, r : r + 1],
+                scalar1=means[:, r : r + 1],
                 scalar2=rstd[:, r : r + 1],
-                op0=ALU.add,
+                op0=ALU.subtract,
                 op1=ALU.mult,
             )
             normed[tile] = n
@@ -409,23 +408,29 @@ def tile_clawmatrix_pa_t_kernel(
         def exponentiate(batch, r):
             neg_logits, neg_max = logits[(batch, r)]
             probs = prob_pool.tile([P, S], F32, tag="probs")
-            row_sum = soft_pool.tile([P, 1], F32, tag="row_sum")
+            if r % PAIR == 0:
+                pair_sums = soft_pool.tile([P, PAIR], F32, tag="row_sums")
+                row_sums[(batch, r // PAIR)] = pair_sums
             nc.scalar.activation(
                 out=probs[:],
                 in_=neg_logits[:],
                 func=ACT.Exp,
                 bias=neg_max[:],
                 scale=-1.0,
-                accum_out=row_sum[:],
+                accum_out=row_sums[(batch, r // PAIR)][:, r % PAIR : r % PAIR + 1],
             )
-            inverse = soft_pool.tile([P, 1], F32, tag="inverse")
-            nc.gpsimd.tensor_tensor(out=inverse[:], in0=row_sum[:], in1=neg_one[:], op=ALU.pow)
-            exponentials[(batch, r)] = (probs, inverse)
+            exponentials[(batch, r)] = probs
+
+        def invert(batch, r):
+            pair_inverses = soft_pool.tile([P, PAIR], F32, tag="inverses")
+            nc.vector.reciprocal(out=pair_inverses[:], in_=row_sums[(batch, r // PAIR)][:])
+            inverses[(batch, r // PAIR)] = pair_inverses
 
         def store_probabilities(batch, r):
-            probs, inverse = exponentials[(batch, r)]
+            probs = exponentials[(batch, r)]
+            inverse = inverses[(batch, r // PAIR)][:, r % PAIR : r % PAIR + 1]
             nc.vector.tensor_scalar(
-                out=probs[:], in0=probs[:], scalar1=inverse[:], scalar2=None, op0=ALU.mult
+                out=probs[:], in0=probs[:], scalar1=inverse, scalar2=None, op0=ALU.mult
             )
             nc.sync.dma_start(out=out[batch, r * P : (r + 1) * P, :], in_=probs[:])
 
@@ -489,19 +494,23 @@ def tile_clawmatrix_pa_t_kernel(
                     finish_scale()
                 for tile in tile_at(step - LAG_SQUARE):
                     square(tile)
-                    if tile % TILES == TILES - 1:
-                        statistics(tile // TILES)
                 for tile in tile_at(step):
                     group_features(tile)
-                for batch, r in sim_at(step - LAG_EXP):
-                    exponentiate(batch, r)
                 for group, t in plane_at(step - LAG_RELU):
                     rectify_plane(group, t)
+                for batch, r in sim_at(step - LAG_EXP):
+                    exponentiate(batch, r)
                 if step == 5:
                     prepare_gains()
                 if 2 <= step < 2 + TILES:
                     for piece in (2 * step - 4, 2 * step - 3):
                         group_weight(1, piece // W_PARTS, piece % W_PARTS, nc.vector.tensor_copy)
+                for tile in tile_at(step - LAG_STATS):
+                    if tile % TILES == TILES - 1:
+                        statistics(tile // TILES)
+                for batch, r in sim_at(step - LAG_INVERT):
+                    if r % PAIR == PAIR - 1:
+                        invert(batch, r)
                 for tile in tile_at(step - LAG_SUM):
                     add_bias(tile)
                 for batch, r in sim_at(step - LAG_LOGITS):

@@ -34,16 +34,16 @@ LAG_PROJECT = 2
 LAG_SUM = 3
 LAG_SQUARE = 4
 LAG_STATS = 5
-LAG_NORM = 9
-LAG_TURN = 13
-LAG_RELU = 13
-LAG_REGROUP = 18
-LAG_YQUANT = 19
-LAG_SIM = 20
-LAG_LOGITS = 21
-LAG_EXP = 22
-LAG_INVERT = 24
-LAG_STORE = 28
+LAG_NORM = 10
+LAG_TURN = 14
+LAG_RELU = 14
+LAG_REGROUP = 19
+LAG_YQUANT = 20
+LAG_SIM = 21
+LAG_LOGITS = 22
+LAG_EXP = 23
+LAG_INVERT = 25
+LAG_STORE = 29
 LOAD_AHEAD = 8
 PAIR = 2
 W_PARTS = 4

from contextlib import ExitStack

import concourse.mybir as mybir
from concourse.masks import make_identity

F32 = mybir.dt.float32
BF16 = mybir.dt.bfloat16
U32 = mybir.dt.uint32
U8 = mybir.dt.uint8
FP8X4 = mybir.dt.float8_e4m3fn_x4
ALU = mybir.AluOpType
ACT = mybir.ActivationFunctionType
AXIS_X = mybir.AxisListType.X

B, S, K, D = 8, 512, 1024, 512
EPS = 1e-5
TEMPERATURE = 0.07

P = 128
PACK = 4
K_PASS = P * PACK
PASSES = K // K_PASS
TILES = S // P
STREAMS = 2
LANGUAGE, VISION = 0, 1
GROUPS = B * STREAMS
ALL_TILES = GROUPS * TILES
WORDS = K // 2

FLOPS = 2 * STREAMS * B * S * K * D + 2 * B * S * S * D

LAG_QUANT = 2
LAG_PROJECT = 2
LAG_SUM = 3
LAG_SQUARE = 4
LAG_STATS = 5
LAG_NORM = 10
LAG_TURN = 14
LAG_RELU = 14
LAG_REGROUP = 19
LAG_YQUANT = 20
LAG_SIM = 21
LAG_LOGITS = 22
LAG_EXP = 23
LAG_INVERT = 25
LAG_STORE = 29
LOAD_AHEAD = 8
PAIR = 2
W_PARTS = 4


def tile_clawmatrix_pa_t_kernel(
    tc, vision_features, language_features, vW, vb, vg, vbeta, lW, lb, lg, lbeta, claw, out
):
    nc = tc.nc
    features = [language_features, vision_features]
    weights = [lW, vW]
    biases = [lb, vb]

    with ExitStack() as ctx:
        const = ctx.enter_context(tc.tile_pool(name="const", bufs=1))
        setup = ctx.enter_context(tc.tile_pool(name="setup", bufs=STREAMS * PASSES))
        x_pool = ctx.enter_context(tc.tile_pool(name="x", bufs=3))
        x0_pool = ctx.enter_context(tc.tile_pool(name="x0", bufs=TILES))
        xq_pool = ctx.enter_context(tc.tile_pool(name="xq", bufs=6))
        z_pool = ctx.enter_context(tc.tile_pool(name="z", bufs=10))
        n_pool = ctx.enter_context(tc.tile_pool(name="n", bufs=12))
        stat_pool = ctx.enter_context(tc.tile_pool(name="stat", bufs=4))
        scrap_pool = ctx.enter_context(tc.tile_pool(name="scrap", bufs=8))
        y_pool = ctx.enter_context(tc.tile_pool(name="y", bufs=3))
        yq_pool = ctx.enter_context(tc.tile_pool(name="yq", bufs=4))
        soft_pool = ctx.enter_context(tc.tile_pool(name="soft", bufs=4))
        prob_pool = ctx.enter_context(tc.tile_pool(name="prob", bufs=16))
        psum = ctx.enter_context(tc.psum_pool(name="psum", bufs=2))

        x_loaded, x_turned, x_grouped, x_quantised = {}, {}, {}, {}
        w_loaded, w_grouped, w_quantised = {}, {}, {}
        projected, summed, sums, stats, normed = {}, {}, {}, {}, {}
        turned, planes, y_grouped, y_quantised = {}, {}, {}, {}
        sims, logits, exponentials, row_sums, inverses = {}, {}, {}, {}, {}

        def regroup_on_scalar(tile):
            return tile + LAG_REGROUP >= ALL_TILES + TILES and tile % TILES == TILES - 1

        def chunk_of(tile):
            first = tile - tile % PAIR
            return (tile, 1) if first + LAG_REGROUP >= ALL_TILES else (first, PAIR)

        def load_features(first, count):
            group, r = divmod(first, TILES)
            batch, stream = divmod(group, STREAMS)
            pool = x0_pool if count == 1 else x_pool
            x_in = pool.tile([P, count, K], BF16, tag="x_in%d" % count)
            nc.sync.dma_start(
                out=x_in[:],
                in_=features[stream][batch, r * P : (r + count) * P, :].rearrange(
                    "(i p) k -> p i k", p=P
                ),
            )
            for i in range(count):
                x_loaded[first + i] = x_in[:, i, :]

        def load_weight(stream, g):
            w_raw = setup.tile([P, PACK * D], BF16, tag="w_raw")
            nc.sync.dma_start(
                out=w_raw[:].rearrange("q (u c) -> q u c", c=2 * D),
                in_=weights[stream][g * K_PASS : (g + 1) * K_PASS, :].rearrange(
                    "(u q e) c -> q u (e c)", q=P, e=2
                ),
            )
            w_loaded[(stream, g)] = w_raw

        ident = const.tile([P, P], F32)
        make_identity(nc, ident[:])
        ones = const.tile([P, P], BF16)
        nc.gpsimd.memset(ones[:], 1.0)
        eps_row = const.tile([P, 2 * TILES], F32)
        nc.vector.memset(eps_row[:, 0:TILES], 0.0)
        nc.vector.memset(eps_row[:, TILES : 2 * TILES], D * D * EPS)
        neg_half = const.tile([P, TILES], F32)
        nc.gpsimd.memset(neg_half[:], -0.5)
        bias_pad = const.tile([P, STREAMS * D], BF16)
        nc.vector.memset(bias_pad[:], 0.0)
        gain_rows = const.tile([P, P], BF16)
        nc.vector.memset(gain_rows[:], 0.0)
        bias_rows = const.tile([P, STREAMS * D], F32)
        gains = const.tile([P, 4 * PACK], F32)
        neg_scale = const.tile([P, 1], F32)
        claw_sb = const.tile([P, D * D // P], BF16)

        def load_vectors():
            for stream in range(STREAMS):
                nc.sync.dma_start(
                    out=bias_pad[0:1, stream * D : (stream + 1) * D],
                    in_=biases[stream].rearrange("(o c) -> o c", o=1),
                )
            for j, vector in enumerate([lg, lbeta, vg, vbeta]):
                nc.sync.dma_start(
                    out=gain_rows[PACK * j : PACK * (j + 1), :],
                    in_=vector.rearrange("(t c) -> t c", t=PACK),
                )

        def spread_biases():
            for stream in range(STREAMS):
                cols = slice(stream * D, (stream + 1) * D)
                spread = psum.tile([P, D], F32, tag="sim")
                nc.tensor.matmul(
                    out=spread[:], lhsT=ones[:], rhs=bias_pad[:, cols], start=True, stop=True
                )
                nc.scalar.copy(out=bias_rows[:, cols], in_=spread[:])

        def prepare_gains():
            gain_rows_f32 = const.tile([P, P], F32)
            nc.scalar.copy(out=gain_rows_f32[:], in_=gain_rows[:])
            gains_ps = psum.tile([P, P], F32, tag="yt")
            nc.tensor.transpose(out=gains_ps[:], in_=gain_rows_f32[:], identity=ident[:])
            used = gains_ps[:, 0 : 4 * PACK].rearrange("p (m j t) -> p m j t", m=STREAMS, j=2)
            kept = gains[:].rearrange("p (m j t) -> p m j t", m=STREAMS, j=2)
            nc.scalar.activation(
                out=kept[:, :, 0, :], in_=used[:, :, 0, :], func=ACT.Copy, scale=1.0 * D
            )
            nc.scalar.copy(out=kept[:, :, 1, :], in_=used[:, :, 1, :])

        claw_columns = []

        def prepare_scale():
            columns = psum.tile([P, D], F32, tag="sim")
            chunks = D // P
            for a in range(chunks):
                nc.tensor.matmul(
                    out=columns[:],
                    lhsT=ones[:],
                    rhs=claw_sb[:, a * D : (a + 1) * D],
                    start=(a == 0),
                    stop=(a == chunks - 1),
                )
            claw_columns.append(columns)

        def finish_scale():
            claw_sum = const.tile([P, 1], F32)
            nc.vector.tensor_reduce(out=claw_sum[:], in_=claw_columns[0][:], axis=AXIS_X, op=ALU.add)
            nc.gpsimd.tensor_scalar(
                out=neg_scale[:],
                in0=claw_sum[:],
                scalar1=-1.0 / (D * D * TEMPERATURE),
                scalar2=None,
                op0=ALU.mult,
            )

        def group_weight(stream, g, part, copy):
            if part == 0:
                wg = setup.tile([P, D * PACK], BF16, tag="w_grouped", align_bytes=64)
                w_grouped[(stream, g)] = wg
            width = D // W_PARTS
            raw = w_loaded[(stream, g)][:].rearrange("p (t c) -> p t c", t=PACK)[
                :, :, part * width : (part + 1) * width
            ]
            copy(
                out=w_grouped[(stream, g)][
                    :, part * width * PACK : (part + 1) * width * PACK
                ].rearrange("p (c i t) -> p c t i", i=4, t=PACK),
                in_=raw.rearrange("p t (c i) -> p c t i", i=4),
            )

        def quantise_weight(stream, g):
            if g == 0:
                w_codes = const.tile(
                    [P, PASSES * D], U32, name="w_codes%d" % stream, align_bytes=64
                )
                w_scales = const.tile(
                    [P, PASSES * D], U8, name="w_scales%d" % stream, align_bytes=64
                )
                w_quantised[stream] = (w_codes, w_scales)
            codes, scales = w_quantised[stream]
            nc.vector.quantize_mx(
                out=codes[:, g * D : (g + 1) * D].bitcast(FP8X4),
                scales=scales[:, g * D : (g + 1) * D],
                in_=w_grouped[(stream, g)][:],
            )

        def transpose_features(tile):
            x_words = x_loaded[tile].bitcast(F32)
            xt = psum.tile([P, WORDS], F32, tag="xt")
            for j in range(WORDS // P):
                nc.tensor.transpose(
                    out=xt[:, j * P : (j + 1) * P],
                    in_=x_words[:, j * P : (j + 1) * P],
                    identity=ident[:],
                )
            x_turned[tile] = xt

        def group_features(tile):
            xg = xq_pool.tile([P, K], BF16, tag="x_grouped", align_bytes=64)
            nc.scalar.copy(
                out=xg[:].bitcast(F32).rearrange("p (g c u) -> p g c u", g=PASSES, u=2),
                in_=x_turned[tile][:].rearrange("p (g u c) -> p g c u", g=PASSES, u=2),
            )
            x_grouped[tile] = xg

        def quantise_features(tile):
            codes = xq_pool.tile([P, PASSES * P], U32, tag="x_codes", align_bytes=64)
            scales = xq_pool.tile([P, PASSES * P], U8, tag="x_scales", align_bytes=64)
            nc.vector.quantize_mx(
                out=codes[:].bitcast(FP8X4), scales=scales[:], in_=x_grouped[tile][:]
            )
            x_quantised[tile] = (codes, scales)

        def project(tile):
            stream = (tile // TILES) % STREAMS
            w_codes, w_scales = w_quantised[stream]
            codes, scales = x_quantised[tile]
            h = psum.tile([P, D], F32, tag="h")
            for g in range(PASSES):
                nc.tensor.matmul_mx(
                    out=h[:],
                    lhsT=codes[:, g * P : (g + 1) * P].bitcast(FP8X4),
                    lhsT_scale=scales[:, g * P : (g + 1) * P],
                    rhs=w_codes[:, g * D : (g + 1) * D].bitcast(FP8X4),
                    rhs_scale=w_scales[:, g * D : (g + 1) * D],
                    start=(g == 0),
                    stop=(g == PASSES - 1),
                )
            projected[tile] = h

        def add_bias(tile):
            stream = (tile // TILES) % STREAMS
            group, r = divmod(tile, TILES)
            if r == 0:
                group_sums = stat_pool.tile([P, 2 * TILES], F32, tag="sums")
                sums[group] = group_sums
            z = z_pool.tile([P, D], F32, tag="z")
            nc.vector.scalar_tensor_tensor(
                out=z[:],
                in0=projected[tile][:],
                scalar=1.0,
                in1=bias_rows[:, stream * D : (stream + 1) * D],
                op0=ALU.mult,
                op1=ALU.add,
                accum_out=sums[group][:, r : r + 1],
            )
            summed[tile] = z

        def square(tile):
            group, r = divmod(tile, TILES)
            squares = scrap_pool.tile([P, D], BF16, tag="squares")
            nc.scalar.activation(
                out=squares[:],
                in_=summed[tile][:],
                func=ACT.Square,
                bias=sums[group][:, r : r + 1],
                scale=-1.0 * D,
                accum_out=sums[group][:, TILES + r : TILES + r + 1],
            )

        def statistics(group):
            means = stat_pool.tile([P, 2 * TILES], F32, tag="means")
            nc.vector.scalar_tensor_tensor(
                out=means[:],
                in0=sums[group][:],
                scalar=1.0 / D,
                in1=eps_row[:],
                op0=ALU.mult,
                op1=ALU.add,
            )
            rstd = stat_pool.tile([P, TILES], F32, tag="rstd")
            nc.gpsimd.tensor_tensor(
                out=rstd[:], in0=means[:, TILES : 2 * TILES], in1=neg_half[:], op=ALU.pow
            )
            stats[group] = (means, rstd)

        def normalise(tile):
            group, r = divmod(tile, TILES)
            means, rstd = stats[group]
            n = n_pool.tile([P, D], F32, tag="normed")
            nc.vector.tensor_scalar(
                out=n[:],
                in0=summed[tile][:],
                scalar1=means[:, r : r + 1],
                scalar2=rstd[:, r : r + 1],
                op0=ALU.subtract,
                op1=ALU.mult,
            )
            normed[tile] = n

        def transpose_plane(group, t):
            yt = psum.tile([P, S], F32, tag="yt")
            for r in range(TILES):
                nc.tensor.transpose(
                    out=yt[:, r * P : (r + 1) * P],
                    in_=normed[group * TILES + r][:, t * P : (t + 1) * P],
                    identity=ident[:],
                )
            turned[(group, t)] = yt

        def rectify_plane(group, t):
            first = 2 * PACK * (group % STREAMS)
            if t == 0:
                y_planes = y_pool.tile([P, PACK, S], BF16, tag="planes")
                planes[group] = y_planes
            nc.scalar.activation(
                out=planes[group][:, t, :],
                in_=turned[(group, t)][:],
                func=ACT.Relu,
                bias=gains[:, first + PACK + t : first + PACK + t + 1],
                scale=gains[:, first + t : first + t + 1],
            )

        def regroup(tile):
            first, count = chunk_of(tile)
            if tile != first + count - 1:
                return
            group, r = divmod(first, TILES)
            yg = y_pool.tile([P, PAIR * P * PACK], BF16, tag="y_grouped", align_bytes=64)
            copy = nc.scalar.copy if regroup_on_scalar(tile) else nc.vector.tensor_copy
            copy(
                out=yg[:, 0 : count * P * PACK].rearrange("p (c i t) -> p c t i", i=4, t=PACK),
                in_=planes[group][:, :, r * P : (r + count) * P].rearrange(
                    "p t (c i) -> p c t i", i=4
                ),
            )
            y_grouped[first] = yg

        def quantise_rectified(tile):
            first, count = chunk_of(tile)
            if tile != first + count - 1:
                return
            group, r = divmod(first, TILES)
            if r == 0:
                y_codes = yq_pool.tile([P, S], U32, tag="y_codes", align_bytes=64)
                y_scales = yq_pool.tile([P, S], U8, tag="y_scales", align_bytes=64)
                y_quantised[group] = (y_codes, y_scales)
            codes, scales = y_quantised[group]
            nc.vector.quantize_mx(
                out=codes[:, r * P : (r + count) * P].bitcast(FP8X4),
                scales=scales[:, r * P : (r + count) * P],
                in_=y_grouped[first][:, 0 : count * P * PACK],
            )

        def similarity(batch, r):
            v_codes, v_scales = y_quantised[STREAMS * batch + VISION]
            l_codes, l_scales = y_quantised[STREAMS * batch + LANGUAGE]
            sim = psum.tile([P, S], F32, tag="sim")
            nc.tensor.matmul_mx(
                out=sim[:],
                lhsT=v_codes[:, r * P : (r + 1) * P].bitcast(FP8X4),
                lhsT_scale=v_scales[:, r * P : (r + 1) * P],
                rhs=l_codes[:].bitcast(FP8X4),
                rhs_scale=l_scales[:],
                start=True,
                stop=True,
            )
            sims[(batch, r)] = sim

        def scale_logits(batch, r):
            neg_logits = soft_pool.tile([P, S], F32, tag="neg_logits")
            neg_max = soft_pool.tile([P, 1], F32, tag="neg_max")
            nc.vector.tensor_scalar(
                out=neg_logits[:],
                in0=sims[(batch, r)][:],
                scalar1=neg_scale[:],
                scalar2=None,
                op0=ALU.mult,
                op1=ALU.min,
                accum_out=neg_max[:],
            )
            logits[(batch, r)] = (neg_logits, neg_max)

        def exponentiate(batch, r):
            neg_logits, neg_max = logits[(batch, r)]
            probs = prob_pool.tile([P, S], F32, tag="probs")
            if r % PAIR == 0:
                pair_sums = soft_pool.tile([P, PAIR], F32, tag="row_sums")
                row_sums[(batch, r // PAIR)] = pair_sums
            nc.scalar.activation(
                out=probs[:],
                in_=neg_logits[:],
                func=ACT.Exp,
                bias=neg_max[:],
                scale=-1.0,
                accum_out=row_sums[(batch, r // PAIR)][:, r % PAIR : r % PAIR + 1],
            )
            exponentials[(batch, r)] = probs

        def invert(batch, r):
            pair_inverses = soft_pool.tile([P, PAIR], F32, tag="inverses")
            nc.vector.reciprocal(out=pair_inverses[:], in_=row_sums[(batch, r // PAIR)][:])
            inverses[(batch, r // PAIR)] = pair_inverses

        def store_probabilities(batch, r):
            probs = exponentials[(batch, r)]
            inverse = inverses[(batch, r // PAIR)][:, r % PAIR : r % PAIR + 1]
            nc.vector.tensor_scalar(
                out=probs[:], in0=probs[:], scalar1=inverse, scalar2=None, op0=ALU.mult
            )
            nc.sync.dma_start(out=out[batch, r * P : (r + 1) * P, :], in_=probs[:])

        def tile_at(step):
            return [step] if 0 <= step < ALL_TILES else []

        def plane_at(step):
            return [divmod(step, TILES)] if 0 <= step < ALL_TILES else []

        def sim_at(step):
            batch, rest = divmod(step - TILES, STREAMS * TILES)
            return [(batch, rest // 2)] if 0 <= batch < B and rest % 2 == 0 else []

        with tc.manual_schedule():
            load_weight(0, 0)
            load_vectors()
            load_weight(0, 1)
            for tile in range(TILES):
                load_features(tile, 1)
            for g in range(PASSES):
                load_weight(1, g)
            for first in range(TILES, LOAD_AHEAD, TILES):
                load_features(first, TILES)
            nc.sync.dma_start(out=claw_sb[:], in_=claw.rearrange("(p a) c -> p (a c)", p=P))

            for step in range(ALL_TILES + LAG_STORE + TILES):
                if step == 0:
                    spread_biases()
                for tile in tile_at(step):
                    transpose_features(tile)
                for group, t in plane_at(step - LAG_TURN):
                    transpose_plane(group, t)
                if step == 0:
                    for part in range(W_PARTS):
                        group_weight(0, 0, part, nc.vector.tensor_copy)
                    for part in range(W_PARTS // 2):
                        group_weight(0, 1, part, nc.vector.tensor_copy)
                    for part in range(W_PARTS // 2, W_PARTS):
                        group_weight(0, 1, part, nc.scalar.copy)
                    quantise_weight(0, 0)
                    quantise_weight(0, 1)
                if step in (4, 6):
                    quantise_weight(1, (step - 4) // 2)
                for tile in tile_at(step - LAG_QUANT):
                    quantise_features(tile)
                for tile in tile_at(step - LAG_NORM):
                    normalise(tile)
                for tile in tile_at(step - LAG_REGROUP):
                    regroup(tile)
                for batch, r in sim_at(step - LAG_STORE):
                    store_probabilities(batch, r)
                for tile in tile_at(step - LAG_YQUANT):
                    quantise_rectified(tile)
                for tile in tile_at(step - LAG_PROJECT):
                    project(tile)
                for batch, r in sim_at(step - LAG_SIM):
                    similarity(batch, r)
                if step == LAG_TURN - 4:
                    prepare_scale()
                if step == LAG_TURN - 2:
                    finish_scale()
                for tile in tile_at(step - LAG_SQUARE):
                    square(tile)
                for tile in tile_at(step):
                    group_features(tile)
                for group, t in plane_at(step - LAG_RELU):
                    rectify_plane(group, t)
                for batch, r in sim_at(step - LAG_EXP):
                    exponentiate(batch, r)
                if step == 5:
                    prepare_gains()
                if 2 <= step < 2 + TILES:
                    for piece in (2 * step - 4, 2 * step - 3):
                        group_weight(1, piece // W_PARTS, piece % W_PARTS, nc.vector.tensor_copy)
                for tile in tile_at(step - LAG_STATS):
                    if tile % TILES == TILES - 1:
                        statistics(tile // TILES)
                for batch, r in sim_at(step - LAG_INVERT):
                    if r % PAIR == PAIR - 1:
                        invert(batch, r)
                for tile in tile_at(step - LAG_SUM):
                    add_bias(tile)
                for batch, r in sim_at(step - LAG_LOGITS):
                    scale_logits(batch, r)
                for first in tile_at(step + LOAD_AHEAD):
                    if first % TILES == 0:
                        load_features(first, TILES)
